import numpy as np
import ml_dtypes


BF16 = ml_dtypes.bfloat16


def bf(x):
    return np.asarray(x, np.float32).astype(BF16)


def f64(x):
    return np.asarray(x).astype(np.float64)


E2M1 = np.array([0.0, 0.5, 1.0, 1.5, 2.0, 3.0, 4.0, 6.0, -0.0, -0.5, -1.0, -1.5, -2.0, -3.0, -4.0, -6.0])


def pack_weight(w, fmt):
    k, n = w.shape
    w = f64(bf(w)).reshape(k // 32, 32, n)
    amax = np.abs(w).max(1)
    if fmt == "e4m3":
        byte = np.frexp(amax)[1] - 1 + 127 - 7
    else:
        mant, ex = np.frexp(amax / 6.0)
        byte = np.where(mant > 0.5, ex, ex - 1) + 127
    byte = np.clip(np.where(amax > 0, byte, 1), 1, 254)
    scaled = (w * np.exp2(127.0 - byte)[:, None, :]).reshape(k, n).astype(np.float32)
    by_word = np.ascontiguousarray(scaled.reshape(k // 512, 128, 4, n).transpose(0, 1, 3, 2))
    if fmt == "e4m3":
        words = by_word.astype(ml_dtypes.float8_e4m3fn).view(np.uint8)
    else:
        c = by_word.astype(ml_dtypes.float4_e2m1fn).view(np.uint8) & 0xF
        words = c[..., 0::2] | (c[..., 1::2] << 4)
    return np.ascontiguousarray(words), np.ascontiguousarray(byte.astype(np.uint8).reshape(k // 512, 16, n))


def unpack_weight(words, scales, fmt):
    g, p, n, _ = words.shape
    if fmt == "e4m3":
        vals = np.ascontiguousarray(words).view(ml_dtypes.float8_e4m3fn).astype(np.float64)
    else:
        nib = np.empty((g, p, n, 4), np.uint8)
        nib[..., 0::2] = words & 0xF
        nib[..., 1::2] = words >> 4
        vals = E2M1[nib]
    vals = vals * np.repeat(np.exp2(scales.astype(np.float64) - 127.0), 8, axis=1)[..., None]
    return vals.transpose(0, 1, 3, 2).reshape(g * 512, n)

def pack4(w):
    words, scales = pack_weight(w, "e2m1")
    return words.reshape(words.shape[0], 128, -1), scales


def unpack4(words, scales):
    return unpack_weight(words.reshape(words.shape[0], 128, -1, 2), scales, "e2m1")


def kspread(k):
    return np.exp2(np.repeat(np.random.randint(-6, 7, k // 32), 32).astype(np.float64))


B, N, K, H, C_E, M = 2, 128, 16, 1536, 1536, 4096
SCALE = 30.0


def setup_inputs():
    s = kspread(M)
    h2 = np.random.standard_normal((B, N, K, M)) * 0.65 * s
    h2_words, h2_scales = pack4(h2.reshape(B * N * K, M).T)
    h_V = bf(np.random.standard_normal((B, N, H)))
    mask_attend = bf(np.random.uniform(size=(B, N, K)) < 0.9)
    words, scales = pack4(np.random.standard_normal((M, H)) * 4.0 / np.sqrt(M) / s[:, None])
    W3_b = bf(np.random.standard_normal(H) * 0.1)
    return {"h2_words": h2_words,
            "h2_scales": h2_scales,
            "h_V": h_V,
            "mask_attend": mask_attend,
            "W3_w_words": words,
            "W3_w_scales": scales,
            "W3_b": W3_b}


def reference(h2_words, h2_scales, h_V, mask_attend, W3_w_words, W3_w_scales, W3_b):
    h2 = unpack4(h2_words, h2_scales).T.reshape(B, N, K, M)
    h_message = (h2 @ unpack4(W3_w_words, W3_w_scales)) + f64(W3_b)
    h_message = f64(mask_attend)[..., None] * h_message
    dh = np.sum(h_message, axis=-2) / SCALE
    return f64(h_V) + dh

@@ -1,0 +1,241 @@
+from contextlib import ExitStack
+
+import concourse.mybir as mybir
+from concourse.masks import make_identity
+
+F32 = mybir.dt.float32
+BF16 = mybir.dt.bfloat16
+I32 = mybir.dt.int32
+U8 = mybir.dt.uint8
+FP4X4 = mybir.dt.float4_e2m1fn_x4
+ALU = mybir.AluOpType
+
+P = 128
+M = 4096
+H = 1536
+EDGES = 4096
+K = 16
+NODES = EDGES // K
+SCALE = 30.0
+
+G = M // 512
+CHUNK = 512
+CHUNKS = EDGES // CHUNK
+CHUNK_NODES = CHUNK // K
+HB = H // P
+HB_A = 8
+Q4 = 32
+
+FLOPS = 2 * M * EDGES * H
+
+
+def tile_declayerj_pb_kernel(tc, h2_words, h2_scales, h_V, mask_attend, W3_w_words, W3_w_scales, W3_b, out):
+    nc = tc.nc
+    hv_flat = h_V.flatten_outer_dims()
+    out_flat = out.flatten_outer_dims()
+    mask_flat = mask_attend.rearrange("b n e -> (b n e)")
+
+    with ExitStack() as ctx:
+        keep = ctx.enter_context(tc.tile_pool(name="keep", bufs=1))
+        work = ctx.enter_context(tc.tile_pool(name="work", bufs=3))
+        psum = ctx.enter_context(tc.psum_pool(name="psum", bufs=8))
+
+        x_codes = []
+        x_planes = []
+        for c in range(CHUNKS):
+            x_codes.append(keep.tile([P, G, 2 * CHUNK], U8, name="xc%d" % c, align_bytes=256))
+            x_planes.append(keep.tile([P, G, CHUNK], U8, name="xp%d" % c, align_bytes=256))
+        w_codes = []
+        w_planes = []
+        for i, blocks in enumerate((HB_A, HB - HB_A)):
+            w_codes.append(keep.tile([P, G, 2 * P * blocks], U8, name="wc%d" % i, align_bytes=256))
+            w_planes.append(keep.tile([P, G, P * blocks], U8, name="wp%d" % i, align_bytes=256))
+        mask_a = keep.tile([P, 2 * CHUNK], BF16, name="mask_a")
+        mask_b = keep.tile([P, EDGES - 2 * CHUNK], BF16, name="mask_b")
+        mask_row = keep.tile([P, 2 * CHUNK], BF16, name="mask_row")
+        bias_rows = keep.tile([P, P], BF16, name="bias_rows")
+        bias = keep.tile([P, HB], F32, name="bias")
+        ones = keep.tile([P, P], BF16, name="ones")
+        ident = keep.tile([P, P], BF16, name="ident")
+        hv = []
+        for c in range(CHUNKS):
+            hv.append(keep.tile([P, HB, Q4], BF16, name="hv%d" % c))
+
+        def zero(plane, g0, g1):
+            nc.vector.memset(plane[:, g0:g1, :].rearrange("p g n -> p (g n)").bitcast(I32), 0)
+
+        def load_codes(tile, words, n0, n1, g0, g1):
+            nc.sync.dma_start(
+                out=tile[:, g0:g1, :].bitcast(I32),
+                in_=words[g0:g1, :, 2 * n0 : 2 * n1].rearrange("g p n -> p g n").bitcast(I32),
+            )
+
+        def load_scales(plane, scales, n0, n1, g0, g1):
+            for q in range(4):
+                nc.sync.dma_start(
+                    out=plane[Q4 * q : Q4 * q + 4, g0:g1, :].bitcast(I32),
+                    in_=scales[g0:g1, 4 * q : 4 * q + 4, n0:n1].rearrange("g r n -> r g n").bitcast(I32),
+                )
+
+        def x_load(c, g0, g1):
+            load_codes(x_codes[c], h2_words, c * CHUNK, (c + 1) * CHUNK, g0, g1)
+
+        def xs_load(c, g0, g1):
+            load_scales(x_planes[c], h2_scales, c * CHUNK, (c + 1) * CHUNK, g0, g1)
+
+        w_range = ((0, P * HB_A), (P * HB_A, H))
+
+        def w_load(i, g0, g1):
+            load_codes(w_codes[i], W3_w_words, w_range[i][0], w_range[i][1], g0, g1)
+
+        def ws_load(i, g0, g1):
+            load_scales(w_planes[i], W3_w_scales, w_range[i][0], w_range[i][1], g0, g1)
+
+        def mx_pass(acc, c, hb, g, e0, e1):
+            i, b = (0, hb) if hb < HB_A else (1, hb - HB_A)
+            nc.tensor.matmul_mx(
+                out=acc,
+                lhsT=w_codes[i][:, g, 2 * P * b : 2 * P * (b + 1)].bitcast(FP4X4),
+                lhsT_scale=w_planes[i][:, g, P * b : P * (b + 1)],
+                rhs=x_codes[c][:, g, 2 * e0 : 2 * e1].bitcast(FP4X4),
+                rhs_scale=x_planes[c][:, g, e0:e1],
+                start=(g == 0),
+                stop=(g == G - 1),
+            )
+
+        def mask_of(c, e0, e1):
+            if c < 2:
+                return mask_a[:, c * CHUNK + e0 : c * CHUNK + e1]
+            return mask_b[:, (c - 2) * CHUNK + e0 : (c - 2) * CHUNK + e1]
+
+        def reduce_edges(acc, sums, c, hb, e0, e1):
+            masked = work.tile([P, CHUNK], F32, name="masked")
+            nc.vector.scalar_tensor_tensor(
+                out=masked[:, : e1 - e0],
+                in0=acc,
+                scalar=bias[:, hb : hb + 1],
+                in1=mask_of(c, e0, e1),
+                op0=ALU.add,
+                op1=ALU.mult,
+            )
+            nc.vector.tensor_reduce(
+                out=sums[:, hb, e0 // K : e1 // K],
+                in_=masked[:, : e1 - e0].rearrange("p (n e) -> p n e", e=K),
+                axis=mybir.AxisListType.X,
+                op=ALU.add,
+            )
+
+        def turn(turned, sums, b0, b1):
+            nc.vector.transpose(
+                out=turned[:, b0:b1, :].rearrange("p b n -> p (b n)"),
+                in_=sums[:, b0:b1, :].rearrange("p b n -> p (b n)"),
+            )
+
+        def residual_and_store(turned, result, c, b0, b1, engines):
+            nc.vector.scalar_tensor_tensor(
+                out=result[:, b0:b1, :].rearrange("p b n -> p (b n)"),
+                in0=turned[:, b0:b1, :].rearrange("p b n -> p (b n)"),
+                scalar=1.0 / SCALE,
+                in1=hv[c][:, b0:b1, :].rearrange("p b n -> p (b n)"),
+                op0=ALU.mult,
+                op1=ALU.add,
+            )
+            rows = out_flat[c * CHUNK_NODES : (c + 1) * CHUNK_NODES, :].rearrange("i (b a j) -> a i b j", a=4, j=Q4)
+            for a in range(4):
+                engines[a].dma_start(out=rows[a][:, b0:b1, :], in_=result[Q4 * a : Q4 * (a + 1), b0:b1, :])
+
+        with tc.manual_schedule(
+            engines={mybir.EngineType.PE, mybir.EngineType.DVE, mybir.EngineType.SP, mybir.EngineType.Pool}
+        ):
+            nc.gpsimd.memset(mask_row[:], 0.0)
+            nc.gpsimd.dma_start(out=mask_row[0:1, :], in_=mask_flat[0 : 2 * CHUNK].rearrange("(o n) -> o n", o=1))
+            nc.gpsimd.memset(bias_rows[:], 0.0)
+            nc.gpsimd.dma_start(out=bias_rows[0:HB, :], in_=W3_b.rearrange("(b p) -> b p", p=P))
+            nc.gpsimd.memset(ones[:], 1.0)
+            make_identity(nc, ident[:])
+            for c in range(CHUNKS):
+                rows = hv_flat[c * CHUNK_NODES : (c + 1) * CHUNK_NODES, :].rearrange("i (b a j) -> a i b j", a=4, j=Q4)
+                for a in range(4):
+                    nc.gpsimd.dma_start(out=hv[c][Q4 * a : Q4 * (a + 1), :, :], in_=rows[a])
+
+            zero(x_planes[0], 0, 2)
+            zero(w_planes[0], 0, 2)
+            zero(x_planes[0], 2, G)
+            zero(w_planes[0], 2, G)
+            zero(w_planes[1], 0, G)
+            for c in range(1, CHUNKS):
+                zero(x_planes[c], 0, G)
+
+            x_load(0, 0, 1)
+            w_load(0, 0, 1)
+            xs_load(0, 0, 2)
+            ws_load(0, 0, 2)
+            x_load(0, 1, 3)
+            w_load(0, 1, 3)
+            xs_load(0, 2, G)
+            ws_load(0, 2, G)
+            x_load(0, 3, 5)
+            w_load(0, 3, 5)
+            x_load(0, 5, G)
+            w_load(0, 5, G)
+            w_load(1, 0, G)
+            ws_load(1, 0, G)
+            for c in range(1, CHUNKS):
+                x_load(c, 0, G)
+                xs_load(c, 0, G)
+                if c == 2:
+                    nc.sync.dma_start(out=mask_b[:], in_=mask_flat[2 * CHUNK :].partition_broadcast(P))
+
+            for c in range(2):
+                acc = psum.tile([P, CHUNK], F32, name="acc")
+                nc.tensor.matmul(
+                    out=acc[:], lhsT=ones[:], rhs=mask_row[:, c * CHUNK : (c + 1) * CHUNK], start=True, stop=True
+                )
+                nc.scalar.copy(out=mask_a[:, c * CHUNK : (c + 1) * CHUNK], in_=acc[:])
+            acc = psum.tile([P, P], BF16, name="acc")
+            nc.tensor.transpose(out=acc[:], in_=bias_rows[:], identity=ident[:])
+            nc.scalar.copy(out=bias[:], in_=acc[:, 0:HB])
+
+            store_engines = (nc.sync, nc.sync, nc.sync, nc.sync)
+            last_engines = (nc.sync, nc.scalar, nc.sync, nc.scalar)
+
+            for c in range(CHUNKS):
+                last = c == CHUNKS - 1
+                sums = work.tile([P, HB, Q4], F32, name="sums", align_bytes=64)
+                turned = work.tile([P, HB, Q4], F32, name="turned", align_bytes=64)
+                result = work.tile([P, HB, Q4], F32, name="result", align_bytes=64)
+
+                first_single = 0
+                if c == 0:
+                    accs = []
+                    for hb in range(HB_A):
+                        acc = psum.tile([P, CHUNK], F32, name="acc")
+                        accs.append(acc)
+                    for g in range(G):
+                        for hb in range(HB_A):
+                            mx_pass(accs[hb][:], c, hb, g, 0, CHUNK)
+                    for hb in range(HB_A):
+                        reduce_edges(accs[hb][:], sums, c, hb, 0, CHUNK)
+                    first_single = HB_A
+                    turn(turned, sums, 0, HB_A)
+
+                for hb in range(first_single, HB):
+                    pieces = ((0, 256), (256, 384), (384, 512)) if last and hb == HB - 1 else ((0, CHUNK),)
+                    for e0, e1 in pieces:
+                        acc = psum.tile([P, CHUNK], F32, name="acc")
+                        for g in range(G):
+                            mx_pass(acc[:, : e1 - e0], c, hb, g, e0, e1)
+                        reduce_edges(acc[:, : e1 - e0], sums, c, hb, e0, e1)
+                    if hb == HB_A - 1:
+                        turn(turned, sums, 0, HB_A)
+                        if last:
+                            residual_and_store(turned, result, c, 0, HB_A, store_engines)
+                    elif last and hb >= HB_A:
+                        turn(turned, sums, hb, hb + 1)
+                        if hb == HB - 2:
+                            residual_and_store(turned, result, c, HB_A, HB - 1, store_engines)
+                        elif hb == HB - 1:
+                            residual_and_store(turned, result, c, HB - 1, HB, last_engines)
+                if not last:
+                    turn(turned, sums, HB_A, HB)
+                    residual_and_store(turned, result, c, 0, HB, store_engines)

@@ -17,6 +17,7 @@ EDGES = 4096
 K = 16
 NODES = EDGES // K
 SCALE = 30.0
+WARM_UP = 3
 
 G = M // 512
 CHUNK = 512
@@ -52,10 +53,9 @@ def tile_declayerj_pb_kernel(tc, h2_words, h2_scales, h_V, mask_attend, W3_w_wor
             w_planes.append(keep.tile([P, G, P * blocks], U8, name="wp%d" % i, align_bytes=256))
         mask_a = keep.tile([P, 2 * CHUNK], BF16, name="mask_a")
         mask_b = keep.tile([P, EDGES - 2 * CHUNK], BF16, name="mask_b")
-        mask_row = keep.tile([P, 2 * CHUNK], BF16, name="mask_row")
+        mask_rows = keep.tile([P, CHUNK], BF16, name="mask_rows")
         bias_rows = keep.tile([P, P], BF16, name="bias_rows")
         bias = keep.tile([P, HB], F32, name="bias")
-        ones = keep.tile([P, P], BF16, name="ones")
         ident = keep.tile([P, P], BF16, name="ident")
         hv = []
         for c in range(CHUNKS):
@@ -90,6 +90,11 @@ def tile_declayerj_pb_kernel(tc, h2_words, h2_scales, h_V, mask_attend, W3_w_wor
 
         def ws_load(i, g0, g1):
             load_scales(w_planes[i], W3_w_scales, w_range[i][0], w_range[i][1], g0, g1)
+
+        def hv_load(c):
+            rows = hv_flat[c * CHUNK_NODES : (c + 1) * CHUNK_NODES, :].rearrange("i (b a j) -> a i b j", a=4, j=Q4)
+            for a in range(4):
+                nc.sync.dma_start(out=hv[c][Q4 * a : Q4 * (a + 1), :, :], in_=rows[a])
 
         def mx_pass(acc, c, hb, g, e0, e1):
             i, b = (0, hb) if hb < HB_A else (1, hb - HB_A)
@@ -147,16 +152,13 @@ def tile_declayerj_pb_kernel(tc, h2_words, h2_scales, h_V, mask_attend, W3_w_wor
         with tc.manual_schedule(
             engines={mybir.EngineType.PE, mybir.EngineType.DVE, mybir.EngineType.SP, mybir.EngineType.Pool}
         ):
-            nc.gpsimd.memset(mask_row[:], 0.0)
-            nc.gpsimd.dma_start(out=mask_row[0:1, :], in_=mask_flat[0 : 2 * CHUNK].rearrange("(o n) -> o n", o=1))
-            nc.gpsimd.memset(bias_rows[:], 0.0)
-            nc.gpsimd.dma_start(out=bias_rows[0:HB, :], in_=W3_b.rearrange("(b p) -> b p", p=P))
-            nc.gpsimd.memset(ones[:], 1.0)
+            nc.gpsimd.memset(mask_rows[:].bitcast(F32), 0.0)
+            nc.scalar.dma_start(
+                out=mask_rows[0:2, :], in_=mask_flat[0 : 2 * CHUNK].rearrange("(c n) -> c n", n=CHUNK)
+            )
             make_identity(nc, ident[:])
-            for c in range(CHUNKS):
-                rows = hv_flat[c * CHUNK_NODES : (c + 1) * CHUNK_NODES, :].rearrange("i (b a j) -> a i b j", a=4, j=Q4)
-                for a in range(4):
-                    nc.gpsimd.dma_start(out=hv[c][Q4 * a : Q4 * (a + 1), :, :], in_=rows[a])
+            nc.gpsimd.memset(bias_rows[:].bitcast(F32), 0.0)
+            nc.gpsimd.dma_start(out=bias_rows[0:HB, :], in_=W3_b.rearrange("(b p) -> b p", p=P))
 
             zero(x_planes[0], 0, 2)
             zero(w_planes[0], 0, 2)
@@ -183,15 +185,23 @@ def tile_declayerj_pb_kernel(tc, h2_words, h2_scales, h_V, mask_attend, W3_w_wor
             for c in range(1, CHUNKS):
                 x_load(c, 0, G)
                 xs_load(c, 0, G)
-                if c == 2:
+                if c == 1:
+                    hv_load(0)
+                    hv_load(1)
+                if c == 3:
                     nc.sync.dma_start(out=mask_b[:], in_=mask_flat[2 * CHUNK :].partition_broadcast(P))
+            for c in range(2, CHUNKS):
+                hv_load(c)
 
             for c in range(2):
                 acc = psum.tile([P, CHUNK], F32, name="acc")
                 nc.tensor.matmul(
-                    out=acc[:], lhsT=ones[:], rhs=mask_row[:, c * CHUNK : (c + 1) * CHUNK], start=True, stop=True
+                    out=acc[:], lhsT=ident[:, c : c + 1].to_broadcast([P, P]), rhs=mask_rows[:], start=True, stop=True
                 )
                 nc.scalar.copy(out=mask_a[:, c * CHUNK : (c + 1) * CHUNK], in_=acc[:])
+            acc = psum.tile([P, CHUNK], F32, name="acc")
+            for i in range(WARM_UP):
+                nc.tensor.matmul(out=acc[:], lhsT=ident[:], rhs=mask_rows[:], start=True, stop=True)
             acc = psum.tile([P, P], BF16, name="acc")
             nc.tensor.transpose(out=acc[:], in_=bias_rows[:], identity=ident[:])
             nc.scalar.copy(out=bias[:], in_=acc[:, 0:HB])
@@ -220,7 +230,7 @@ def tile_declayerj_pb_kernel(tc, h2_words, h2_scales, h_V, mask_attend, W3_w_wor
                     turn(turned, sums, 0, HB_A)
 
                 for hb in range(first_single, HB):
-                    pieces = ((0, 256), (256, 384), (384, 512)) if last and hb == HB - 1 else ((0, CHUNK),)
+                    pieces = ((0, 256), (256, 512)) if last and hb == HB - 1 else ((0, CHUNK),)
                     for e0, e1 in pieces:
                         acc = psum.tile([P, CHUNK], F32, name="acc")
                         for g in range(G):
@@ -232,10 +242,10 @@ def tile_declayerj_pb_kernel(tc, h2_words, h2_scales, h_V, mask_attend, W3_w_wor
                             residual_and_store(turned, result, c, 0, HB_A, store_engines)
                     elif last and hb >= HB_A:
                         turn(turned, sums, hb, hb + 1)
-                        if hb == HB - 2:
-                            residual_and_store(turned, result, c, HB_A, HB - 1, store_engines)
+                        if hb == HB - 3:
+                            residual_and_store(turned, result, c, HB_A, HB - 2, store_engines)
                         elif hb == HB - 1:
-                            residual_and_store(turned, result, c, HB - 1, HB, last_engines)
+                            residual_and_store(turned, result, c, HB - 2, HB, last_engines)
                 if not last:
                     turn(turned, sums, HB_A, HB)
                     residual_and_store(turned, result, c, 0, HB, store_engines)

@@ -1,4 +1,5 @@
 from contextlib import ExitStack
+from functools import partial
 
 import concourse.mybir as mybir
 from concourse.masks import make_identity
@@ -39,7 +40,8 @@ def tile_declayerj_pb_kernel(tc, h2_words, h2_scales, h_V, mask_attend, W3_w_wor
     with ExitStack() as ctx:
         keep = ctx.enter_context(tc.tile_pool(name="keep", bufs=1))
         work = ctx.enter_context(tc.tile_pool(name="work", bufs=3))
-        psum = ctx.enter_context(tc.psum_pool(name="psum", bufs=8))
+        products = ctx.enter_context(tc.tile_pool(name="products", bufs=10))
+        psum = ctx.enter_context(tc.psum_pool(name="psum", bufs=1))
 
         x_codes = []
         x_planes = []
@@ -113,8 +115,12 @@ def tile_declayerj_pb_kernel(tc, h2_words, h2_scales, h_V, mask_attend, W3_w_wor
                 return mask_a[:, c * CHUNK + e0 : c * CHUNK + e1]
             return mask_b[:, (c - 2) * CHUNK + e0 : (c - 2) * CHUNK + e1]
 
-        def reduce_edges(acc, sums, c, hb, e0, e1):
-            masked = work.tile([P, CHUNK], F32, name="masked")
+        def bank(k, dtype=F32, columns=CHUNK):
+            acc = psum.tile([P, columns], dtype, name="bank%d" % k)
+            return acc
+
+        def mask_edges(acc, c, hb, e0, e1):
+            masked = products.tile([P, CHUNK], F32, name="masked")
             nc.vector.scalar_tensor_tensor(
                 out=masked[:, : e1 - e0],
                 in0=acc,
@@ -123,6 +129,9 @@ def tile_declayerj_pb_kernel(tc, h2_words, h2_scales, h_V, mask_attend, W3_w_wor
                 op0=ALU.add,
                 op1=ALU.mult,
             )
+            return masked
+
+        def sum_edges(masked, sums, hb, e0, e1):
             nc.vector.tensor_reduce(
                 out=sums[:, hb, e0 // K : e1 // K],
                 in_=masked[:, : e1 - e0].rearrange("p (n e) -> p n e", e=K),
@@ -194,20 +203,34 @@ def tile_declayerj_pb_kernel(tc, h2_words, h2_scales, h_V, mask_attend, W3_w_wor
                 hv_load(c)
 
             for c in range(2):
-                acc = psum.tile([P, CHUNK], F32, name="acc")
+                acc = bank(7 - c)
                 nc.tensor.matmul(
                     out=acc[:], lhsT=ident[:, c : c + 1].to_broadcast([P, P]), rhs=mask_rows[:], start=True, stop=True
                 )
                 nc.scalar.copy(out=mask_a[:, c * CHUNK : (c + 1) * CHUNK], in_=acc[:])
-            acc = psum.tile([P, CHUNK], F32, name="acc")
+            acc = bank(5)
             for i in range(WARM_UP):
                 nc.tensor.matmul(out=acc[:], lhsT=ident[:], rhs=mask_rows[:], start=True, stop=True)
-            acc = psum.tile([P, P], BF16, name="acc")
+            acc = bank(4, BF16, P)
             nc.tensor.transpose(out=acc[:], in_=bias_rows[:], identity=ident[:])
             nc.scalar.copy(out=bias[:], in_=acc[:, 0:HB])
 
+            order = []
+            even, odd = [0, 3, 2, 1], [7, 6, 5, 4]
+            while len(order) < CHUNKS * HB:
+                order.extend(even)
+                order.extend(odd)
+                even, odd = even[::-1], odd[::-1]
+
             store_engines = (nc.sync, nc.sync, nc.sync, nc.sync)
             last_engines = (nc.sync, nc.scalar, nc.sync, nc.scalar)
+            waiting = []
+            count = 0
+
+            def run_waiting():
+                for step in waiting:
+                    step()
+                waiting.clear()
 
             for c in range(CHUNKS):
                 last = c == CHUNKS - 1
@@ -217,35 +240,41 @@ def tile_declayerj_pb_kernel(tc, h2_words, h2_scales, h_V, mask_attend, W3_w_wor
 
                 first_single = 0
                 if c == 0:
-                    accs = []
-                    for hb in range(HB_A):
-                        acc = psum.tile([P, CHUNK], F32, name="acc")
-                        accs.append(acc)
+                    accs = [bank(hb) for hb in range(HB_A)]
                     for g in range(G):
                         for hb in range(HB_A):
                             mx_pass(accs[hb][:], c, hb, g, 0, CHUNK)
+                    masked = [mask_edges(accs[hb][:], c, hb, 0, CHUNK) for hb in range(HB_A)]
                     for hb in range(HB_A):
-                        reduce_edges(accs[hb][:], sums, c, hb, 0, CHUNK)
-                    first_single = HB_A
+                        sum_edges(masked[hb], sums, hb, 0, CHUNK)
                     turn(turned, sums, 0, HB_A)
+                    first_single = HB_A
 
                 for hb in range(first_single, HB):
                     pieces = ((0, 256), (256, 512)) if last and hb == HB - 1 else ((0, CHUNK),)
                     for e0, e1 in pieces:
-                        acc = psum.tile([P, CHUNK], F32, name="acc")
+                        acc = bank(order[count])
+                        count += 1
                         for g in range(G):
                             mx_pass(acc[:, : e1 - e0], c, hb, g, e0, e1)
-                        reduce_edges(acc[:, : e1 - e0], sums, c, hb, e0, e1)
+                        product = mask_edges(acc[:, : e1 - e0], c, hb, e0, e1)
+                        run_waiting()
+                        waiting.append(partial(sum_edges, product, sums, hb, e0, e1))
+                        if last and hb >= HB - 3:
+                            run_waiting()
                     if hb == HB_A - 1:
-                        turn(turned, sums, 0, HB_A)
+                        waiting.append(partial(turn, turned, sums, 0, HB_A))
                         if last:
-                            residual_and_store(turned, result, c, 0, HB_A, store_engines)
+                            waiting.append(partial(residual_and_store, turned, result, c, 0, HB_A, store_engines))
                     elif last and hb >= HB_A:
-                        turn(turned, sums, hb, hb + 1)
+                        waiting.append(partial(turn, turned, sums, hb, hb + 1))
                         if hb == HB - 3:
-                            residual_and_store(turned, result, c, HB_A, HB - 2, store_engines)
+                            waiting.append(
+                                partial(residual_and_store, turned, result, c, HB_A, HB - 2, store_engines)
+                            )
                         elif hb == HB - 1:
-                            residual_and_store(turned, result, c, HB - 2, HB, last_engines)
+                            waiting.append(partial(residual_and_store, turned, result, c, HB - 2, HB, last_engines))
                 if not last:
-                    turn(turned, sums, HB_A, HB)
-                    residual_and_store(turned, result, c, 0, HB, store_engines)
+                    waiting.append(partial(turn, turned, sums, HB_A, HB))
+                    waiting.append(partial(residual_and_store, turned, result, c, 0, HB, store_engines))
+            run_waiting()

@@ -181,14 +181,18 @@ def tile_declayerj_pb_kernel(tc, h2_words, h2_scales, h_V, mask_attend, W3_w_wor
             w_load(0, 0, 1)
             xs_load(0, 0, 2)
             ws_load(0, 0, 2)
-            x_load(0, 1, 3)
-            w_load(0, 1, 3)
-            xs_load(0, 2, G)
-            ws_load(0, 2, G)
-            x_load(0, 3, 5)
-            w_load(0, 3, 5)
-            x_load(0, 5, G)
-            w_load(0, 5, G)
+            for g0, g1 in ((1, 2), (2, 3)):
+                x_load(0, g0, g1)
+                w_load(0, g0, g1)
+            xs_load(0, 2, 4)
+            ws_load(0, 2, 4)
+            x_load(0, 3, 4)
+            w_load(0, 3, 4)
+            for g0 in (4, 6):
+                x_load(0, g0, g0 + 2)
+                w_load(0, g0, g0 + 2)
+                xs_load(0, g0, g0 + 2)
+                ws_load(0, g0, g0 + 2)
             w_load(1, 0, G)
             ws_load(1, 0, G)
             for c in range(1, CHUNKS):

from contextlib import ExitStack
from functools import partial

import concourse.mybir as mybir
from concourse.masks import make_identity

F32 = mybir.dt.float32
BF16 = mybir.dt.bfloat16
I32 = mybir.dt.int32
U8 = mybir.dt.uint8
FP4X4 = mybir.dt.float4_e2m1fn_x4
ALU = mybir.AluOpType

P = 128
M = 4096
H = 1536
EDGES = 4096
K = 16
NODES = EDGES // K
SCALE = 30.0
WARM_UP = 3

G = M // 512
CHUNK = 512
CHUNKS = EDGES // CHUNK
CHUNK_NODES = CHUNK // K
HB = H // P
HB_A = 8
Q4 = 32

FLOPS = 2 * M * EDGES * H


def tile_declayerj_pb_kernel(tc, h2_words, h2_scales, h_V, mask_attend, W3_w_words, W3_w_scales, W3_b, out):
    nc = tc.nc
    hv_flat = h_V.flatten_outer_dims()
    out_flat = out.flatten_outer_dims()
    mask_flat = mask_attend.rearrange("b n e -> (b n e)")

    with ExitStack() as ctx:
        keep = ctx.enter_context(tc.tile_pool(name="keep", bufs=1))
        work = ctx.enter_context(tc.tile_pool(name="work", bufs=3))
        products = ctx.enter_context(tc.tile_pool(name="products", bufs=10))
        psum = ctx.enter_context(tc.psum_pool(name="psum", bufs=1))

        x_codes = []
        x_planes = []
        for c in range(CHUNKS):
            x_codes.append(keep.tile([P, G, 2 * CHUNK], U8, name="xc%d" % c, align_bytes=256))
            x_planes.append(keep.tile([P, G, CHUNK], U8, name="xp%d" % c, align_bytes=256))
        w_codes = []
        w_planes = []
        for i, blocks in enumerate((HB_A, HB - HB_A)):
            w_codes.append(keep.tile([P, G, 2 * P * blocks], U8, name="wc%d" % i, align_bytes=256))
            w_planes.append(keep.tile([P, G, P * blocks], U8, name="wp%d" % i, align_bytes=256))
        mask_a = keep.tile([P, 2 * CHUNK], BF16, name="mask_a")
        mask_b = keep.tile([P, EDGES - 2 * CHUNK], BF16, name="mask_b")
        mask_rows = keep.tile([P, CHUNK], BF16, name="mask_rows")
        bias_rows = keep.tile([P, P], BF16, name="bias_rows")
        bias = keep.tile([P, HB], F32, name="bias")
        ident = keep.tile([P, P], BF16, name="ident")
        hv = []
        for c in range(CHUNKS):
            hv.append(keep.tile([P, HB, Q4], BF16, name="hv%d" % c))

        def zero(plane, g0, g1):
            nc.vector.memset(plane[:, g0:g1, :].rearrange("p g n -> p (g n)").bitcast(I32), 0)

        def load_codes(tile, words, n0, n1, g0, g1):
            nc.sync.dma_start(
                out=tile[:, g0:g1, :].bitcast(I32),
                in_=words[g0:g1, :, 2 * n0 : 2 * n1].rearrange("g p n -> p g n").bitcast(I32),
            )

        def load_scales(plane, scales, n0, n1, g0, g1):
            for q in range(4):
                nc.sync.dma_start(
                    out=plane[Q4 * q : Q4 * q + 4, g0:g1, :].bitcast(I32),
                    in_=scales[g0:g1, 4 * q : 4 * q + 4, n0:n1].rearrange("g r n -> r g n").bitcast(I32),
                )

        def x_load(c, g0, g1):
            load_codes(x_codes[c], h2_words, c * CHUNK, (c + 1) * CHUNK, g0, g1)

        def xs_load(c, g0, g1):
            load_scales(x_planes[c], h2_scales, c * CHUNK, (c + 1) * CHUNK, g0, g1)

        w_range = ((0, P * HB_A), (P * HB_A, H))

        def w_load(i, g0, g1):
            load_codes(w_codes[i], W3_w_words, w_range[i][0], w_range[i][1], g0, g1)

        def ws_load(i, g0, g1):
            load_scales(w_planes[i], W3_w_scales, w_range[i][0], w_range[i][1], g0, g1)

        def hv_load(c):
            rows = hv_flat[c * CHUNK_NODES : (c + 1) * CHUNK_NODES, :].rearrange("i (b a j) -> a i b j", a=4, j=Q4)
            for a in range(4):
                nc.sync.dma_start(out=hv[c][Q4 * a : Q4 * (a + 1), :, :], in_=rows[a])

        def mx_pass(acc, c, hb, g, e0, e1):
            i, b = (0, hb) if hb < HB_A else (1, hb - HB_A)
            nc.tensor.matmul_mx(
                out=acc,
                lhsT=w_codes[i][:, g, 2 * P * b : 2 * P * (b + 1)].bitcast(FP4X4),
                lhsT_scale=w_planes[i][:, g, P * b : P * (b + 1)],
                rhs=x_codes[c][:, g, 2 * e0 : 2 * e1].bitcast(FP4X4),
                rhs_scale=x_planes[c][:, g, e0:e1],
                start=(g == 0),
                stop=(g == G - 1),
            )

        def mask_of(c, e0, e1):
            if c < 2:
                return mask_a[:, c * CHUNK + e0 : c * CHUNK + e1]
            return mask_b[:, (c - 2) * CHUNK + e0 : (c - 2) * CHUNK + e1]

        def bank(k, dtype=F32, columns=CHUNK):
            acc = psum.tile([P, columns], dtype, name="bank%d" % k)
            return acc

        def mask_edges(acc, c, hb, e0, e1):
            masked = products.tile([P, CHUNK], F32, name="masked")
            nc.vector.scalar_tensor_tensor(
                out=masked[:, : e1 - e0],
                in0=acc,
                scalar=bias[:, hb : hb + 1],
                in1=mask_of(c, e0, e1),
                op0=ALU.add,
                op1=ALU.mult,
            )
            return masked

        def sum_edges(masked, sums, hb, e0, e1):
            nc.vector.tensor_reduce(
                out=sums[:, hb, e0 // K : e1 // K],
                in_=masked[:, : e1 - e0].rearrange("p (n e) -> p n e", e=K),
                axis=mybir.AxisListType.X,
                op=ALU.add,
            )

        def turn(turned, sums, b0, b1):
            nc.vector.transpose(
                out=turned[:, b0:b1, :].rearrange("p b n -> p (b n)"),
                in_=sums[:, b0:b1, :].rearrange("p b n -> p (b n)"),
            )

        def residual_and_store(turned, result, c, b0, b1, engines):
            nc.vector.scalar_tensor_tensor(
                out=result[:, b0:b1, :].rearrange("p b n -> p (b n)"),
                in0=turned[:, b0:b1, :].rearrange("p b n -> p (b n)"),
                scalar=1.0 / SCALE,
                in1=hv[c][:, b0:b1, :].rearrange("p b n -> p (b n)"),
                op0=ALU.mult,
                op1=ALU.add,
            )
            rows = out_flat[c * CHUNK_NODES : (c + 1) * CHUNK_NODES, :].rearrange("i (b a j) -> a i b j", a=4, j=Q4)
            for a in range(4):
                engines[a].dma_start(out=rows[a][:, b0:b1, :], in_=result[Q4 * a : Q4 * (a + 1), b0:b1, :])

        with tc.manual_schedule(
            engines={mybir.EngineType.PE, mybir.EngineType.DVE, mybir.EngineType.SP, mybir.EngineType.Pool}
        ):
            nc.gpsimd.memset(mask_rows[:].bitcast(F32), 0.0)
            nc.scalar.dma_start(
                out=mask_rows[0:2, :], in_=mask_flat[0 : 2 * CHUNK].rearrange("(c n) -> c n", n=CHUNK)
            )
            make_identity(nc, ident[:])
            nc.gpsimd.memset(bias_rows[:].bitcast(F32), 0.0)
            nc.gpsimd.dma_start(out=bias_rows[0:HB, :], in_=W3_b.rearrange("(b p) -> b p", p=P))

            zero(x_planes[0], 0, 2)
            zero(w_planes[0], 0, 2)
            zero(x_planes[0], 2, G)
            zero(w_planes[0], 2, G)
            zero(w_planes[1], 0, G)
            for c in range(1, CHUNKS):
                zero(x_planes[c], 0, G)

            x_load(0, 0, 1)
            w_load(0, 0, 1)
            xs_load(0, 0, 2)
            ws_load(0, 0, 2)
            for g0, g1 in ((1, 2), (2, 3)):
                x_load(0, g0, g1)
                w_load(0, g0, g1)
            xs_load(0, 2, 4)
            ws_load(0, 2, 4)
            x_load(0, 3, 4)
            w_load(0, 3, 4)
            for g0 in (4, 6):
                x_load(0, g0, g0 + 2)
                w_load(0, g0, g0 + 2)
                xs_load(0, g0, g0 + 2)
                ws_load(0, g0, g0 + 2)
            w_load(1, 0, G)
            ws_load(1, 0, G)
            for c in range(1, CHUNKS):
                x_load(c, 0, G)
                xs_load(c, 0, G)
                if c == 1:
                    hv_load(0)
                    hv_load(1)
                if c == 3:
                    nc.sync.dma_start(out=mask_b[:], in_=mask_flat[2 * CHUNK :].partition_broadcast(P))
            for c in range(2, CHUNKS):
                hv_load(c)

            for c in range(2):
                acc = bank(7 - c)
                nc.tensor.matmul(
                    out=acc[:], lhsT=ident[:, c : c + 1].to_broadcast([P, P]), rhs=mask_rows[:], start=True, stop=True
                )
                nc.scalar.copy(out=mask_a[:, c * CHUNK : (c + 1) * CHUNK], in_=acc[:])
            acc = bank(5)
            for i in range(WARM_UP):
                nc.tensor.matmul(out=acc[:], lhsT=ident[:], rhs=mask_rows[:], start=True, stop=True)
            acc = bank(4, BF16, P)
            nc.tensor.transpose(out=acc[:], in_=bias_rows[:], identity=ident[:])
            nc.scalar.copy(out=bias[:], in_=acc[:, 0:HB])

            order = []
            even, odd = [0, 3, 2, 1], [7, 6, 5, 4]
            while len(order) < CHUNKS * HB:
                order.extend(even)
                order.extend(odd)
                even, odd = even[::-1], odd[::-1]

            store_engines = (nc.sync, nc.sync, nc.sync, nc.sync)
            last_engines = (nc.sync, nc.scalar, nc.sync, nc.scalar)
            waiting = []
            count = 0

            def run_waiting():
                for step in waiting:
                    step()
                waiting.clear()

            for c in range(CHUNKS):
                last = c == CHUNKS - 1
                sums = work.tile([P, HB, Q4], F32, name="sums", align_bytes=64)
                turned = work.tile([P, HB, Q4], F32, name="turned", align_bytes=64)
                result = work.tile([P, HB, Q4], F32, name="result", align_bytes=64)

                first_single = 0
                if c == 0:
                    accs = [bank(hb) for hb in range(HB_A)]
                    for g in range(G):
                        for hb in range(HB_A):
                            mx_pass(accs[hb][:], c, hb, g, 0, CHUNK)
                    masked = [mask_edges(accs[hb][:], c, hb, 0, CHUNK) for hb in range(HB_A)]
                    for hb in range(HB_A):
                        sum_edges(masked[hb], sums, hb, 0, CHUNK)
                    turn(turned, sums, 0, HB_A)
                    first_single = HB_A

                for hb in range(first_single, HB):
                    pieces = ((0, 256), (256, 512)) if last and hb == HB - 1 else ((0, CHUNK),)
                    for e0, e1 in pieces:
                        acc = bank(order[count])
                        count += 1
                        for g in range(G):
                            mx_pass(acc[:, : e1 - e0], c, hb, g, e0, e1)
                        product = mask_edges(acc[:, : e1 - e0], c, hb, e0, e1)
                        run_waiting()
                        waiting.append(partial(sum_edges, product, sums, hb, e0, e1))
                        if last and hb >= HB - 3:
                            run_waiting()
                    if hb == HB_A - 1:
                        waiting.append(partial(turn, turned, sums, 0, HB_A))
                        if last:
                            waiting.append(partial(residual_and_store, turned, result, c, 0, HB_A, store_engines))
                    elif last and hb >= HB_A:
                        waiting.append(partial(turn, turned, sums, hb, hb + 1))
                        if hb == HB - 3:
                            waiting.append(
                                partial(residual_and_store, turned, result, c, HB_A, HB - 2, store_engines)
                            )
                        elif hb == HB - 1:
                            waiting.append(partial(residual_and_store, turned, result, c, HB - 2, HB, last_engines))
                if not last:
                    waiting.append(partial(turn, turned, sums, HB_A, HB))
                    waiting.append(partial(residual_and_store, turned, result, c, 0, HB, store_engines))
            run_waiting()
